import numpy as np
import ml_dtypes


def mxq(x, axis, fmt="e4m3"):
    dtype, down = {"e4m3": (ml_dtypes.float8_e4m3fn, 7), "e5m2": (ml_dtypes.float8_e5m2, 14)}[fmt]
    v = np.moveaxis(np.asarray(x, np.float32).astype(ml_dtypes.bfloat16).astype(np.float64), axis, -1)
    blocks = v.reshape(v.shape[:-1] + (-1, 32))
    amax = np.abs(blocks).max(-1, keepdims=True)
    byte = np.maximum(np.where(amax > 0, np.frexp(amax)[1] - 1 + 127, 0) - down, 1)
    scale = np.exp2(byte - 127.0)
    codes = (blocks / scale).astype(np.float32).astype(dtype).astype(np.float64)
    return np.moveaxis((codes * scale).reshape(v.shape), -1, axis)


WIDE = False


def mx_kscale(k):
    if not WIDE:
        return np.ones(k)
    levels = np.array([10, -10, 5, -5, 0])
    a = np.random.permutation(np.resize(levels, k // 512 * 4)).reshape(k // 512, 4)
    idx = np.arange(k)
    return np.exp2(a[idx // 512, idx % 128 // 32])


BF16 = ml_dtypes.bfloat16


def bf(x):
    return np.asarray(x, np.float32).astype(BF16)


def f64(x):
    return np.asarray(x).astype(np.float64)


E2M1 = np.array([0.0, 0.5, 1.0, 1.5, 2.0, 3.0, 4.0, 6.0, -0.0, -0.5, -1.0, -1.5, -2.0, -3.0, -4.0, -6.0])


def pack_weight(w, fmt):
    k, n = w.shape
    w = f64(bf(w)).reshape(k // 32, 32, n)
    amax = np.abs(w).max(1)
    if fmt == "e4m3":
        byte = np.frexp(amax)[1] - 1 + 127 - 7
    else:
        mant, ex = np.frexp(amax / 6.0)
        byte = np.where(mant > 0.5, ex, ex - 1) + 127
    byte = np.clip(np.where(amax > 0, byte, 1), 1, 254)
    scaled = (w * np.exp2(127.0 - byte)[:, None, :]).reshape(k, n).astype(np.float32)
    by_word = np.ascontiguousarray(scaled.reshape(k // 512, 128, 4, n).transpose(0, 1, 3, 2))
    if fmt == "e4m3":
        words = by_word.astype(ml_dtypes.float8_e4m3fn).view(np.uint8)
    else:
        c = by_word.astype(ml_dtypes.float4_e2m1fn).view(np.uint8) & 0xF
        words = c[..., 0::2] | (c[..., 1::2] << 4)
    return np.ascontiguousarray(words), np.ascontiguousarray(byte.astype(np.uint8).reshape(k // 512, 16, n))


def unpack_weight(words, scales, fmt):
    g, p, n, _ = words.shape
    if fmt == "e4m3":
        vals = np.ascontiguousarray(words).view(ml_dtypes.float8_e4m3fn).astype(np.float64)
    else:
        nib = np.empty((g, p, n, 4), np.uint8)
        nib[..., 0::2] = words & 0xF
        nib[..., 1::2] = words >> 4
        vals = E2M1[nib]
    vals = vals * np.repeat(np.exp2(scales.astype(np.float64) - 127.0), 8, axis=1)[..., None]
    return vals.transpose(0, 1, 3, 2).reshape(g * 512, n)

def pack4(w):
    words, scales = pack_weight(w, "e2m1")
    return words.reshape(words.shape[0], 128, -1), scales


def unpack4(words, scales):
    return unpack_weight(words.reshape(words.shape[0], 128, -1, 2), scales, "e2m1")


N, N_CH, X, H = 4096, 4, 512, 256
K = N_CH * H


def sigmoid(v):
    return 1.0 / (1.0 + np.exp(-v))


def setup_inputs():
    s, t = mx_kscale(X), mx_kscale(K)
    x = bf(np.random.standard_normal((N, X)) * s)
    x_mask = bf(np.random.random(N) < 0.75)
    neighbour_h = bf(np.random.standard_normal((N, N_CH, H)) * t.reshape(N_CH, H))
    neighbour_c = bf(np.random.standard_normal((N, N_CH, H)))
    W_f_in_words, W_f_in_scales = pack4(np.random.standard_normal((X, H)) * 0.5 / np.sqrt(X) / s[:, None])
    b_f_in = bf(np.random.standard_normal(H) * 0.3)
    W_aggr_f_words, W_aggr_f_scales = pack4(np.random.standard_normal((K, K)) / np.sqrt(K) / t[:, None])
    b_aggr_f = bf(np.random.standard_normal(K) * 0.3)
    return {
        "x": x,
        "x_mask": x_mask,
        "neighbour_h": neighbour_h,
        "neighbour_c": neighbour_c,
        "W_f_in_words": W_f_in_words,
        "W_f_in_scales": W_f_in_scales,
        "b_f_in": b_f_in,
        "W_aggr_f_words": W_aggr_f_words,
        "W_aggr_f_scales": W_aggr_f_scales,
        "b_aggr_f": b_aggr_f,
    }


def reference(x, x_mask, neighbour_h, neighbour_c, W_f_in_words, W_f_in_scales, b_f_in, W_aggr_f_words, W_aggr_f_scales, b_aggr_f):
    h_flat = f64(neighbour_h).reshape(N, K)
    f_input = ((mxq(f64(x), 1, "e4m3") @ unpack4(W_f_in_words, W_f_in_scales)) + f64(b_f_in)) * f64(x_mask)[:, None]
    f_input = np.tile(f_input, (1, N_CH))
    f_gate = (mxq(h_flat, 1, "e4m3") @ unpack4(W_aggr_f_words, W_aggr_f_scales)) + f64(b_aggr_f) + f_input
    f_aggr = f_gate + f_input
    f = sigmoid(f_aggr).reshape(N, N_CH, H)
    return np.sum(f * f64(neighbour_c), axis=1)

@@ -1,0 +1,236 @@
+from contextlib import ExitStack
+
+import concourse.mybir as mybir
+from concourse.masks import make_identity
+
+F32 = mybir.dt.float32
+BF16 = mybir.dt.bfloat16
+I32 = mybir.dt.int32
+U32 = mybir.dt.uint32
+U8 = mybir.dt.uint8
+FP8X4 = mybir.dt.float8_e4m3fn_x4
+FP4X4 = mybir.dt.float4_e2m1fn_x4
+ADD = mybir.AluOpType.add
+MULT = mybir.AluOpType.mult
+SIGMOID = mybir.ActivationFunctionType.Sigmoid
+
+P = 128
+NODES, X_DIM, CHILDREN, H_DIM = 4096, 512, 4, 256
+HF_DIM = CHILDREN * H_DIM
+K_PASS = 512
+WORDS = K_PASS // 2
+BLOCK = 512
+SUBS = BLOCK // P
+N_BLOCKS = NODES // BLOCK
+GROUPS = 1 + HF_DIM // K_PASS
+HALVES = H_DIM // P
+FEATURE_TILES = CHILDREN * HALVES
+FP4_TILE_BYTES = 2 * P
+PAIR = 2
+
+FLOPS = 2 * NODES * X_DIM * H_DIM + 2 * NODES * HF_DIM * HF_DIM
+
+
+def tile_treelstmcell_pa_t_kernel(
+    tc,
+    x,
+    x_mask,
+    neighbour_h,
+    neighbour_c,
+    W_f_in_words,
+    W_f_in_scales,
+    b_f_in,
+    W_aggr_f_words,
+    W_aggr_f_scales,
+    b_aggr_f,
+    out,
+):
+    nc = tc.nc
+
+    x_blocks = x.rearrange("(b p s) k -> b p s k", p=P, s=SUBS)
+    h_blocks = neighbour_h.rearrange("(b p s) c f -> b p s (c f)", p=P, s=SUBS)
+    c_blocks = neighbour_c.rearrange("(b p s) c f -> b p s c f", p=P, s=SUBS)
+    out_blocks = out.rearrange("(b p s) j -> b p s j", p=P, s=SUBS)
+
+    with ExitStack() as ctx:
+        ctx.enter_context(tc.manual_schedule())
+        const = ctx.enter_context(tc.tile_pool(name="const", bufs=1))
+        loads = ctx.enter_context(tc.tile_pool(name="loads", bufs=3))
+        grouped_pool = ctx.enter_context(tc.tile_pool(name="grouped", bufs=GROUPS))
+        quant_pool = ctx.enter_context(tc.tile_pool(name="quant", bufs=2 * GROUPS))
+        fi_pool = ctx.enter_context(tc.tile_pool(name="fi", bufs=2 * HALVES))
+        z_pool = ctx.enter_context(tc.tile_pool(name="z", bufs=3))
+        gate_pool = ctx.enter_context(tc.tile_pool(name="gate", bufs=FEATURE_TILES))
+        sum_pool = ctx.enter_context(tc.tile_pool(name="sum", bufs=3))
+        out_pool = ctx.enter_context(tc.tile_pool(name="out", bufs=2))
+        psum = ctx.enter_context(tc.psum_pool(name="psum", bufs=8))
+
+        loaded = {}
+        grouped = {}
+        quantised = {}
+
+        def load_block(b):
+            x_sb = loads.tile([P, SUBS, X_DIM], BF16, tag="x")
+            nc.sync.dma_start(out=x_sb[:], in_=x_blocks[b])
+            h_sb = loads.tile([P, SUBS, HF_DIM], BF16, tag="h")
+            nc.sync.dma_start(out=h_sb[:], in_=h_blocks[b])
+            c_sb = loads.tile([P, SUBS, CHILDREN, H_DIM], BF16, tag="c")
+            loaded[b] = (x_sb, h_sb, c_sb)
+
+        def load_cell_states(b):
+            nc.sync.dma_start(out=loaded[b][2][:], in_=c_blocks[b])
+
+        ident = const.tile([P, P], F32)
+        make_identity(nc, ident[:])
+
+        bias_rows = const.tile([P, P], BF16)
+        nc.vector.memset(bias_rows[:], 0.0)
+        wf_scales = const.tile([P, H_DIM], U8, align_bytes=64)
+        nc.vector.memset(wf_scales[:].bitcast(I32), 0)
+        w_scales = const.tile([P, HF_DIM // K_PASS, HF_DIM], U8, align_bytes=64)
+        nc.vector.memset(w_scales[:].bitcast(I32), 0)
+
+        nc.scalar.dma_start(out=bias_rows[0:FEATURE_TILES, :], in_=b_aggr_f.rearrange("(r c) -> r c", c=P))
+        nc.scalar.dma_start(
+            out=bias_rows[FEATURE_TILES : FEATURE_TILES + HALVES, :], in_=b_f_in.rearrange("(r c) -> r c", c=P)
+        )
+
+        load_block(0)
+        for quad in range(4):
+            rows = slice(4 * quad, 4 * quad + 4)
+            parts = slice(32 * quad, 32 * quad + 4)
+            nc.sync.dma_start(out=wf_scales[parts, :].bitcast(I32), in_=W_f_in_scales[0, rows, :].bitcast(I32))
+            nc.sync.dma_start(
+                out=w_scales[parts, :, :].bitcast(I32),
+                in_=W_aggr_f_scales[:, rows, :].rearrange("g r n -> r g n").bitcast(I32),
+            )
+        wf_words = const.tile([P, 2 * H_DIM], U8, align_bytes=64)
+        nc.sync.dma_start(out=wf_words[:].bitcast(I32), in_=W_f_in_words[0].bitcast(I32))
+        w_words = const.tile([P, HF_DIM // K_PASS, 2 * HF_DIM], U8, align_bytes=64)
+        for g in range(HF_DIM // K_PASS):
+            nc.sync.dma_start(out=w_words[:, g, :].bitcast(I32), in_=W_aggr_f_words[g].bitcast(I32))
+        mask_all = const.tile([P, NODES], BF16)
+        nc.sync.dma_start(out=mask_all[:], in_=x_mask.partition_broadcast(P))
+        load_cell_states(0)
+        load_block(1)
+        load_cell_states(1)
+
+        bias_rows_f32 = const.tile([P, P], F32)
+        nc.vector.tensor_copy(out=bias_rows_f32[:], in_=bias_rows[:])
+        bias_bank = psum.tile([P, P], F32, tag="bank")
+        nc.tensor.transpose(bias_bank[:], bias_rows_f32[:], ident[:])
+        bias = const.tile([P, FEATURE_TILES + HALVES], F32)
+        nc.vector.tensor_copy(out=bias[:], in_=bias_bank[:, 0 : FEATURE_TILES + HALVES])
+
+        def transpose_in(b, g, pair):
+            if g == 0:
+                words = loaded[b][0][:].bitcast(F32)
+            else:
+                words = loaded[b][1][:].bitcast(F32)[:, :, WORDS * (g - 1) : WORDS * g]
+            if pair == 0:
+                grouped_tile = grouped_pool.tile([P, 4 * BLOCK], BF16, tag="grouped", align_bytes=64)
+                grouped[g] = grouped_tile
+            bank = psum.tile([P, PAIR, 2, P], F32, tag="bank")
+            for i in range(PAIR):
+                for u in range(2):
+                    nc.tensor.transpose(bank[:, i, u, :], words[:, PAIR * pair + i, u:WORDS:2], ident[:])
+            by_node = grouped[g][:].bitcast(F32).rearrange("p (s n u) -> p s n u", s=SUBS, u=2)
+            nc.scalar.copy(
+                out=by_node[:, PAIR * pair : PAIR * (pair + 1)], in_=bank[:].rearrange("p i u n -> p i n u")
+            )
+
+        def quantise(b, g):
+            codes = quant_pool.tile([P, BLOCK], U32, tag="codes", align_bytes=64)
+            scales = quant_pool.tile([P, BLOCK], U8, tag="scales", align_bytes=64)
+            nc.vector.quantize_mx(out=codes[:].bitcast(FP8X4), scales=scales[:], in_=grouped[g][:])
+            quantised[(b, g)] = (codes, scales)
+
+        def forget_gates(b):
+            mask = mask_all[:, BLOCK * b : BLOCK * (b + 1)].rearrange("q (p s) -> q s p", s=SUBS)
+            fi = {}
+            for half in range(HALVES):
+                codes, scales = quantised[(b, 0)]
+                xw = psum.tile([P, BLOCK], F32, tag="bank")
+                nc.tensor.matmul_mx(
+                    out=xw[:],
+                    lhsT=wf_words[:, FP4_TILE_BYTES * half : FP4_TILE_BYTES * (half + 1)].bitcast(FP4X4),
+                    lhsT_scale=wf_scales[:, P * half : P * (half + 1)],
+                    rhs=codes[:].bitcast(FP8X4),
+                    rhs_scale=scales[:],
+                    start=True,
+                    stop=True,
+                )
+                fi_tile = fi_pool.tile([P, BLOCK], F32, tag="fi")
+                nc.vector.scalar_tensor_tensor(
+                    out=fi_tile[:].rearrange("q (s p) -> q s p", s=SUBS),
+                    in0=xw[:].rearrange("q (s p) -> q s p", s=SUBS),
+                    scalar=bias[:, FEATURE_TILES + half : FEATURE_TILES + half + 1],
+                    in1=mask,
+                    op0=ADD,
+                    op1=MULT,
+                )
+                fi[half] = fi_tile
+            gates = {}
+            for half in range(HALVES):
+                for child in range(CHILDREN):
+                    ft = HALVES * child + half
+                    hw = psum.tile([P, BLOCK], F32, tag="bank")
+                    for g in range(HF_DIM // K_PASS):
+                        codes, scales = quantised[(b, 1 + g)]
+                        nc.tensor.matmul_mx(
+                            out=hw[:],
+                            lhsT=w_words[:, g, FP4_TILE_BYTES * ft : FP4_TILE_BYTES * (ft + 1)].bitcast(FP4X4),
+                            lhsT_scale=w_scales[:, g, P * ft : P * (ft + 1)],
+                            rhs=codes[:].bitcast(FP8X4),
+                            rhs_scale=scales[:],
+                            start=(g == 0),
+                            stop=(g == HF_DIM // K_PASS - 1),
+                        )
+                    z = z_pool.tile([P, BLOCK], F32, tag="z")
+                    nc.vector.scalar_tensor_tensor(out=z[:], in0=fi[half][:], scalar=2.0, in1=hw[:], op0=MULT, op1=ADD)
+                    gate = gate_pool.tile([P, BLOCK], F32, tag="gate")
+                    nc.scalar.activation(out=gate[:], in_=z[:], func=SIGMOID, bias=bias[:, ft : ft + 1], scale=1.0)
+                    gates[(child, half)] = gate
+            return gates
+
+        def gated_sum(b, gates, half, s, products, out_sb):
+            c_sb = loaded[b][2]
+            bank = psum.tile([P, CHILDREN, P], F32, tag="bank")
+            for child in range(CHILDREN):
+                nc.tensor.transpose(bank[:, child, :], gates[(child, half)][:, P * s : P * (s + 1)], ident[:])
+            nc.vector.tensor_tensor(
+                out=products[:, s % PAIR], in0=bank[:], in1=c_sb[:, s, :, P * half : P * (half + 1)], op=MULT
+            )
+            if s % PAIR == PAIR - 1:
+                two = sum_pool.tile([P, PAIR, 2, P], F32, tag="two")
+                nc.gpsimd.tensor_tensor(out=two[:], in0=products[:, :, 0:2, :], in1=products[:, :, 2:4, :], op=ADD)
+                nc.gpsimd.tensor_tensor(
+                    out=out_sb[:, s + 1 - PAIR : s + 1, P * half : P * (half + 1)],
+                    in0=two[:, :, 0, :],
+                    in1=two[:, :, 1, :],
+                    op=ADD,
+                )
+
+        for g in range(GROUPS):
+            for pair in range(SUBS // PAIR):
+                transpose_in(0, g, pair)
+            quantise(0, g)
+
+        for b in range(N_BLOCKS):
+            if b + 2 < N_BLOCKS:
+                load_block(b + 2)
+                load_cell_states(b + 2)
+            gates = forget_gates(b)
+            out_sb = out_pool.tile([P, SUBS, H_DIM], F32, tag="out")
+            products = None
+            for step in range(HALVES * SUBS):
+                half, s = divmod(step, SUBS)
+                if s % PAIR == 0:
+                    products = sum_pool.tile([P, PAIR, CHILDREN, P], F32, tag="products")
+                gated_sum(b, gates, half, s, products, out_sb)
+                if b + 1 < N_BLOCKS:
+                    if step < GROUPS * (SUBS // PAIR):
+                        transpose_in(b + 1, step // (SUBS // PAIR), step % (SUBS // PAIR))
+                    if step >= 2 and step % (SUBS // PAIR) == 0:
+                        quantise(b + 1, step // (SUBS // PAIR) - 1)
+            nc.sync.dma_start(out=out_blocks[b], in_=out_sb[:])

@@ -27,6 +27,7 @@ HALVES = H_DIM // P
 FEATURE_TILES = CHILDREN * HALVES
 FP4_TILE_BYTES = 2 * P
 PAIR = 2
+UNITS = 4
 
 FLOPS = 2 * NODES * X_DIM * H_DIM + 2 * NODES * HF_DIM * HF_DIM
 
@@ -60,25 +61,30 @@ def tile_treelstmcell_pa_t_kernel(
         quant_pool = ctx.enter_context(tc.tile_pool(name="quant", bufs=2 * GROUPS))
         fi_pool = ctx.enter_context(tc.tile_pool(name="fi", bufs=2 * HALVES))
         z_pool = ctx.enter_context(tc.tile_pool(name="z", bufs=3))
-        gate_pool = ctx.enter_context(tc.tile_pool(name="gate", bufs=FEATURE_TILES))
+        gate_pool = ctx.enter_context(tc.tile_pool(name="gate", bufs=12))
         sum_pool = ctx.enter_context(tc.tile_pool(name="sum", bufs=3))
         out_pool = ctx.enter_context(tc.tile_pool(name="out", bufs=2))
         psum = ctx.enter_context(tc.psum_pool(name="psum", bufs=8))
 
-        loaded = {}
+        activations = {}
+        cell_states = {}
         grouped = {}
         quantised = {}
+        input_terms = {}
+        gates = {}
+        results = {}
 
-        def load_block(b):
+        def load_activations(b):
             x_sb = loads.tile([P, SUBS, X_DIM], BF16, tag="x")
             nc.sync.dma_start(out=x_sb[:], in_=x_blocks[b])
             h_sb = loads.tile([P, SUBS, HF_DIM], BF16, tag="h")
             nc.sync.dma_start(out=h_sb[:], in_=h_blocks[b])
-            c_sb = loads.tile([P, SUBS, CHILDREN, H_DIM], BF16, tag="c")
-            loaded[b] = (x_sb, h_sb, c_sb)
+            activations[b] = (x_sb, h_sb)
 
         def load_cell_states(b):
-            nc.sync.dma_start(out=loaded[b][2][:], in_=c_blocks[b])
+            c_sb = loads.tile([P, SUBS, CHILDREN, H_DIM], BF16, tag="c")
+            nc.sync.dma_start(out=c_sb[:], in_=c_blocks[b])
+            cell_states[b] = c_sb
 
         ident = const.tile([P, P], F32)
         make_identity(nc, ident[:])
@@ -95,7 +101,7 @@ def tile_treelstmcell_pa_t_kernel(
             out=bias_rows[FEATURE_TILES : FEATURE_TILES + HALVES, :], in_=b_f_in.rearrange("(r c) -> r c", c=P)
         )
 
-        load_block(0)
+        load_activations(0)
         for quad in range(4):
             rows = slice(4 * quad, 4 * quad + 4)
             parts = slice(32 * quad, 32 * quad + 4)
@@ -111,9 +117,6 @@ def tile_treelstmcell_pa_t_kernel(
             nc.sync.dma_start(out=w_words[:, g, :].bitcast(I32), in_=W_aggr_f_words[g].bitcast(I32))
         mask_all = const.tile([P, NODES], BF16)
         nc.sync.dma_start(out=mask_all[:], in_=x_mask.partition_broadcast(P))
-        load_cell_states(0)
-        load_block(1)
-        load_cell_states(1)
 
         bias_rows_f32 = const.tile([P, P], F32)
         nc.vector.tensor_copy(out=bias_rows_f32[:], in_=bias_rows[:])
@@ -122,22 +125,22 @@ def tile_treelstmcell_pa_t_kernel(
         bias = const.tile([P, FEATURE_TILES + HALVES], F32)
         nc.vector.tensor_copy(out=bias[:], in_=bias_bank[:, 0 : FEATURE_TILES + HALVES])
 
-        def transpose_in(b, g, pair):
+        def transpose_in(b, g):
             if g == 0:
-                words = loaded[b][0][:].bitcast(F32)
+                words = activations[b][0][:].bitcast(F32)
             else:
-                words = loaded[b][1][:].bitcast(F32)[:, :, WORDS * (g - 1) : WORDS * g]
-            if pair == 0:
-                grouped_tile = grouped_pool.tile([P, 4 * BLOCK], BF16, tag="grouped", align_bytes=64)
-                grouped[g] = grouped_tile
-            bank = psum.tile([P, PAIR, 2, P], F32, tag="bank")
-            for i in range(PAIR):
-                for u in range(2):
-                    nc.tensor.transpose(bank[:, i, u, :], words[:, PAIR * pair + i, u:WORDS:2], ident[:])
-            by_node = grouped[g][:].bitcast(F32).rearrange("p (s n u) -> p s n u", s=SUBS, u=2)
-            nc.scalar.copy(
-                out=by_node[:, PAIR * pair : PAIR * (pair + 1)], in_=bank[:].rearrange("p i u n -> p i n u")
-            )
+                words = activations[b][1][:].bitcast(F32)[:, :, WORDS * (g - 1) : WORDS * g]
+            grouped_tile = grouped_pool.tile([P, 4 * BLOCK], BF16, tag="grouped", align_bytes=64)
+            by_node = grouped_tile[:].bitcast(F32).rearrange("p (s n u) -> p s n u", s=SUBS, u=2)
+            for pair in range(SUBS // PAIR):
+                bank = psum.tile([P, PAIR, 2, P], F32, tag="bank")
+                for i in range(PAIR):
+                    for u in range(2):
+                        nc.tensor.transpose(bank[:, i, u, :], words[:, PAIR * pair + i, u:WORDS:2], ident[:])
+                nc.scalar.copy(
+                    out=by_node[:, PAIR * pair : PAIR * (pair + 1)], in_=bank[:].rearrange("p i u n -> p i n u")
+                )
+            grouped[g] = grouped_tile
 
         def quantise(b, g):
             codes = quant_pool.tile([P, BLOCK], U32, tag="codes", align_bytes=64)
@@ -145,11 +148,10 @@ def tile_treelstmcell_pa_t_kernel(
             nc.vector.quantize_mx(out=codes[:].bitcast(FP8X4), scales=scales[:], in_=grouped[g][:])
             quantised[(b, g)] = (codes, scales)
 
-        def forget_gates(b):
+        def input_term(b):
             mask = mask_all[:, BLOCK * b : BLOCK * (b + 1)].rearrange("q (p s) -> q s p", s=SUBS)
-            fi = {}
+            codes, scales = quantised[(b, 0)]
             for half in range(HALVES):
-                codes, scales = quantised[(b, 0)]
                 xw = psum.tile([P, BLOCK], F32, tag="bank")
                 nc.tensor.matmul_mx(
                     out=xw[:],
@@ -160,77 +162,95 @@ def tile_treelstmcell_pa_t_kernel(
                     start=True,
                     stop=True,
                 )
-                fi_tile = fi_pool.tile([P, BLOCK], F32, tag="fi")
+                fi = fi_pool.tile([P, BLOCK], F32, tag="fi")
                 nc.vector.scalar_tensor_tensor(
-                    out=fi_tile[:].rearrange("q (s p) -> q s p", s=SUBS),
+                    out=fi[:].rearrange("q (s p) -> q s p", s=SUBS),
                     in0=xw[:].rearrange("q (s p) -> q s p", s=SUBS),
                     scalar=bias[:, FEATURE_TILES + half : FEATURE_TILES + half + 1],
                     in1=mask,
                     op0=ADD,
                     op1=MULT,
                 )
-                fi[half] = fi_tile
-            gates = {}
-            for half in range(HALVES):
-                for child in range(CHILDREN):
-                    ft = HALVES * child + half
-                    hw = psum.tile([P, BLOCK], F32, tag="bank")
-                    for g in range(HF_DIM // K_PASS):
-                        codes, scales = quantised[(b, 1 + g)]
-                        nc.tensor.matmul_mx(
-                            out=hw[:],
-                            lhsT=w_words[:, g, FP4_TILE_BYTES * ft : FP4_TILE_BYTES * (ft + 1)].bitcast(FP4X4),
-                            lhsT_scale=w_scales[:, g, P * ft : P * (ft + 1)],
-                            rhs=codes[:].bitcast(FP8X4),
-                            rhs_scale=scales[:],
-                            start=(g == 0),
-                            stop=(g == HF_DIM // K_PASS - 1),
-                        )
-                    z = z_pool.tile([P, BLOCK], F32, tag="z")
-                    nc.vector.scalar_tensor_tensor(out=z[:], in0=fi[half][:], scalar=2.0, in1=hw[:], op0=MULT, op1=ADD)
-                    gate = gate_pool.tile([P, BLOCK], F32, tag="gate")
-                    nc.scalar.activation(out=gate[:], in_=z[:], func=SIGMOID, bias=bias[:, ft : ft + 1], scale=1.0)
-                    gates[(child, half)] = gate
-            return gates
+                input_terms[(b, half)] = fi
 
-        def gated_sum(b, gates, half, s, products, out_sb):
-            c_sb = loaded[b][2]
-            bank = psum.tile([P, CHILDREN, P], F32, tag="bank")
-            for child in range(CHILDREN):
-                nc.tensor.transpose(bank[:, child, :], gates[(child, half)][:, P * s : P * (s + 1)], ident[:])
-            nc.vector.tensor_tensor(
-                out=products[:, s % PAIR], in0=bank[:], in1=c_sb[:, s, :, P * half : P * (half + 1)], op=MULT
-            )
-            if s % PAIR == PAIR - 1:
-                two = sum_pool.tile([P, PAIR, 2, P], F32, tag="two")
-                nc.gpsimd.tensor_tensor(out=two[:], in0=products[:, :, 0:2, :], in1=products[:, :, 2:4, :], op=ADD)
-                nc.gpsimd.tensor_tensor(
-                    out=out_sb[:, s + 1 - PAIR : s + 1, P * half : P * (half + 1)],
-                    in0=two[:, :, 0, :],
-                    in1=two[:, :, 1, :],
-                    op=ADD,
+        def forget_gate(b, child, half):
+            ft = HALVES * child + half
+            hw = psum.tile([P, BLOCK], F32, tag="bank")
+            for g in range(HF_DIM // K_PASS):
+                codes, scales = quantised[(b, 1 + g)]
+                nc.tensor.matmul_mx(
+                    out=hw[:],
+                    lhsT=w_words[:, g, FP4_TILE_BYTES * ft : FP4_TILE_BYTES * (ft + 1)].bitcast(FP4X4),
+                    lhsT_scale=w_scales[:, g, P * ft : P * (ft + 1)],
+                    rhs=codes[:].bitcast(FP8X4),
+                    rhs_scale=scales[:],
+                    start=(g == 0),
+                    stop=(g == HF_DIM // K_PASS - 1),
                 )
+            z = z_pool.tile([P, BLOCK], F32, tag="z")
+            nc.vector.scalar_tensor_tensor(
+                out=z[:], in0=input_terms[(b, half)][:], scalar=2.0, in1=hw[:], op0=MULT, op1=ADD
+            )
+            gate = gate_pool.tile([P, BLOCK], F32, tag="gate")
+            nc.scalar.activation(out=gate[:], in_=z[:], func=SIGMOID, bias=bias[:, ft : ft + 1], scale=1.0)
+            gates[(b, child, half)] = gate
 
-        for g in range(GROUPS):
-            for pair in range(SUBS // PAIR):
-                transpose_in(0, g, pair)
-            quantise(0, g)
+        def gated_sum(b, half, pair):
+            products = sum_pool.tile([P, PAIR, CHILDREN, P], F32, tag="products")
+            for i in range(PAIR):
+                s = PAIR * pair + i
+                bank = psum.tile([P, CHILDREN, P], F32, tag="bank")
+                for child in range(CHILDREN):
+                    nc.tensor.transpose(bank[:, child, :], gates[(b, child, half)][:, P * s : P * (s + 1)], ident[:])
+                nc.vector.tensor_tensor(
+                    out=products[:, i], in0=bank[:], in1=cell_states[b][:, s, :, P * half : P * (half + 1)], op=MULT
+                )
+            two = sum_pool.tile([P, PAIR, 2, P], F32, tag="two")
+            nc.gpsimd.tensor_tensor(out=two[:], in0=products[:, :, 0:2, :], in1=products[:, :, 2:4, :], op=ADD)
+            nc.gpsimd.tensor_tensor(
+                out=results[b][:, PAIR * pair : PAIR * (pair + 1), P * half : P * (half + 1)],
+                in0=two[:, :, 0, :],
+                in1=two[:, :, 1, :],
+                op=ADD,
+            )
 
-        for b in range(N_BLOCKS):
-            if b + 2 < N_BLOCKS:
-                load_block(b + 2)
-                load_cell_states(b + 2)
-            gates = forget_gates(b)
-            out_sb = out_pool.tile([P, SUBS, H_DIM], F32, tag="out")
-            products = None
-            for step in range(HALVES * SUBS):
-                half, s = divmod(step, SUBS)
-                if s % PAIR == 0:
-                    products = sum_pool.tile([P, PAIR, CHILDREN, P], F32, tag="products")
-                gated_sum(b, gates, half, s, products, out_sb)
-                if b + 1 < N_BLOCKS:
-                    if step < GROUPS * (SUBS // PAIR):
-                        transpose_in(b + 1, step // (SUBS // PAIR), step % (SUBS // PAIR))
-                    if step >= 2 and step % (SUBS // PAIR) == 0:
-                        quantise(b + 1, step // (SUBS // PAIR) - 1)
-            nc.sync.dma_start(out=out_blocks[b], in_=out_sb[:])
+        def is_block(b):
+            return 0 <= b < N_BLOCKS
+
+        for n in range(-UNITS - 1, UNITS * N_BLOCKS + 2):
+            b, q = divmod(n, UNITS)
+            if q == 3:
+                if is_block(b + 3):
+                    load_activations(b + 3)
+                if is_block(b + 2):
+                    load_cell_states(b + 2)
+
+            if is_block(b):
+                for child in range(PAIR * (q % 2), PAIR * (q % 2) + PAIR):
+                    forget_gate(b, child, q // 2)
+            if q == 2 and is_block(b + 1):
+                input_term(b + 1)
+
+            back_b, back_q = divmod(n - 2, UNITS)
+            if is_block(back_b):
+                if back_q == 0:
+                    out_sb = out_pool.tile([P, SUBS, H_DIM], F32, tag="out")
+                    results[back_b] = out_sb
+                gated_sum(back_b, back_q // 2, back_q % 2)
+                if back_q == UNITS - 1:
+                    nc.sync.dma_start(out=out_blocks[back_b], in_=results[back_b][:])
+
+            if is_block(b + 1):
+                if q == 0:
+                    quantise(b + 1, 0)
+                if q == 1:
+                    quantise(b + 1, 1)
+                if q == 3:
+                    quantise(b + 1, 2)
+
+            if q == 3 and is_block(b + 2):
+                transpose_in(b + 2, 0)
+            if q == 0 and is_block(b + 1):
+                transpose_in(b + 1, 1)
+            if q == 1 and is_block(b + 1):
+                transpose_in(b + 1, 2)

@@ -228,7 +228,7 @@ def tile_treelstmcell_pa_t_kernel(
             if is_block(b):
                 for child in range(PAIR * (q % 2), PAIR * (q % 2) + PAIR):
                     forget_gate(b, child, q // 2)
-            if q == 2 and is_block(b + 1):
+            if q == 3 and is_block(b + 1):
                 input_term(b + 1)
 
             back_b, back_q = divmod(n - 2, UNITS)
@@ -245,7 +245,7 @@ def tile_treelstmcell_pa_t_kernel(
                     quantise(b + 1, 0)
                 if q == 1:
                     quantise(b + 1, 1)
-                if q == 3:
+                if q == 2:
                     quantise(b + 1, 2)
 
             if q == 3 and is_block(b + 2):

@@ -57,6 +57,7 @@ def tile_treelstmcell_pa_t_kernel(
         ctx.enter_context(tc.manual_schedule())
         const = ctx.enter_context(tc.tile_pool(name="const", bufs=1))
         loads = ctx.enter_context(tc.tile_pool(name="loads", bufs=3))
+        sorted_pool = ctx.enter_context(tc.tile_pool(name="sorted", bufs=GROUPS))
         grouped_pool = ctx.enter_context(tc.tile_pool(name="grouped", bufs=GROUPS))
         quant_pool = ctx.enter_context(tc.tile_pool(name="quant", bufs=2 * GROUPS))
         fi_pool = ctx.enter_context(tc.tile_pool(name="fi", bufs=2 * HALVES))
@@ -68,6 +69,7 @@ def tile_treelstmcell_pa_t_kernel(
 
         activations = {}
         cell_states = {}
+        sorted_words = {}
         grouped = {}
         quantised = {}
         input_terms = {}
@@ -125,18 +127,24 @@ def tile_treelstmcell_pa_t_kernel(
         bias = const.tile([P, FEATURE_TILES + HALVES], F32)
         nc.vector.tensor_copy(out=bias[:], in_=bias_bank[:, 0 : FEATURE_TILES + HALVES])
 
-        def transpose_in(b, g):
+        def sort_words(b, g):
             if g == 0:
                 words = activations[b][0][:].bitcast(F32)
             else:
                 words = activations[b][1][:].bitcast(F32)[:, :, WORDS * (g - 1) : WORDS * g]
+            by_parity = sorted_pool.tile([P, SUBS, 2, P], F32, tag="sorted")
+            nc.scalar.copy(out=by_parity[:], in_=words.rearrange("n s (p u) -> n s u p", u=2))
+            sorted_words[g] = by_parity
+
+        def transpose_in(b, g):
+            words = sorted_words[g]
             grouped_tile = grouped_pool.tile([P, 4 * BLOCK], BF16, tag="grouped", align_bytes=64)
             by_node = grouped_tile[:].bitcast(F32).rearrange("p (s n u) -> p s n u", s=SUBS, u=2)
             for pair in range(SUBS // PAIR):
                 bank = psum.tile([P, PAIR, 2, P], F32, tag="bank")
                 for i in range(PAIR):
                     for u in range(2):
-                        nc.tensor.transpose(bank[:, i, u, :], words[:, PAIR * pair + i, u:WORDS:2], ident[:])
+                        nc.tensor.transpose(bank[:, i, u, :], words[:, PAIR * pair + i, u, :], ident[:])
                 nc.scalar.copy(
                     out=by_node[:, PAIR * pair : PAIR * (pair + 1)], in_=bank[:].rearrange("p i u n -> p i n u")
                 )
@@ -217,8 +225,14 @@ def tile_treelstmcell_pa_t_kernel(
         def is_block(b):
             return 0 <= b < N_BLOCKS
 
-        for n in range(-UNITS - 1, UNITS * N_BLOCKS + 2):
+        for n in range(-UNITS - 2, UNITS * N_BLOCKS + 2):
             b, q = divmod(n, UNITS)
+            if q == 2 and is_block(b + 2):
+                sort_words(b + 2, 0)
+            if q == 3 and is_block(b + 2):
+                sort_words(b + 2, 1)
+            if q == 0 and is_block(b + 1):
+                sort_words(b + 1, 2)
             if q == 3:
                 if is_block(b + 3):
                     load_activations(b + 3)

@@ -57,7 +57,6 @@ def tile_treelstmcell_pa_t_kernel(
         ctx.enter_context(tc.manual_schedule())
         const = ctx.enter_context(tc.tile_pool(name="const", bufs=1))
         loads = ctx.enter_context(tc.tile_pool(name="loads", bufs=3))
-        sorted_pool = ctx.enter_context(tc.tile_pool(name="sorted", bufs=GROUPS))
         grouped_pool = ctx.enter_context(tc.tile_pool(name="grouped", bufs=GROUPS))
         quant_pool = ctx.enter_context(tc.tile_pool(name="quant", bufs=2 * GROUPS))
         fi_pool = ctx.enter_context(tc.tile_pool(name="fi", bufs=2 * HALVES))
@@ -69,19 +68,20 @@ def tile_treelstmcell_pa_t_kernel(
 
         activations = {}
         cell_states = {}
-        sorted_words = {}
         grouped = {}
         quantised = {}
         input_terms = {}
         gates = {}
         results = {}
 
-        def load_activations(b):
+        def load_activations(b, queue):
             x_sb = loads.tile([P, SUBS, X_DIM], BF16, tag="x")
-            nc.sync.dma_start(out=x_sb[:], in_=x_blocks[b])
+            queue.dma_start(out=x_sb[:], in_=x_blocks[b])
             h_sb = loads.tile([P, SUBS, HF_DIM], BF16, tag="h")
-            nc.sync.dma_start(out=h_sb[:], in_=h_blocks[b])
-            activations[b] = (x_sb, h_sb)
+            queue.dma_start(out=h_sb[:], in_=h_blocks[b])
+            mask_sb = loads.tile([P, BLOCK], BF16, tag="mask")
+            queue.dma_start(out=mask_sb[:], in_=x_mask[BLOCK * b : BLOCK * (b + 1)].partition_broadcast(P))
+            activations[b] = (x_sb, h_sb, mask_sb)
 
         def load_cell_states(b):
             c_sb = loads.tile([P, SUBS, CHILDREN, H_DIM], BF16, tag="c")
@@ -103,7 +103,7 @@ def tile_treelstmcell_pa_t_kernel(
             out=bias_rows[FEATURE_TILES : FEATURE_TILES + HALVES, :], in_=b_f_in.rearrange("(r c) -> r c", c=P)
         )
 
-        load_activations(0)
+        load_activations(0, nc.scalar)
         for quad in range(4):
             rows = slice(4 * quad, 4 * quad + 4)
             parts = slice(32 * quad, 32 * quad + 4)
@@ -117,8 +117,6 @@ def tile_treelstmcell_pa_t_kernel(
         w_words = const.tile([P, HF_DIM // K_PASS, 2 * HF_DIM], U8, align_bytes=64)
         for g in range(HF_DIM // K_PASS):
             nc.sync.dma_start(out=w_words[:, g, :].bitcast(I32), in_=W_aggr_f_words[g].bitcast(I32))
-        mask_all = const.tile([P, NODES], BF16)
-        nc.sync.dma_start(out=mask_all[:], in_=x_mask.partition_broadcast(P))
 
         bias_rows_f32 = const.tile([P, P], F32)
         nc.vector.tensor_copy(out=bias_rows_f32[:], in_=bias_rows[:])
@@ -127,24 +125,18 @@ def tile_treelstmcell_pa_t_kernel(
         bias = const.tile([P, FEATURE_TILES + HALVES], F32)
         nc.vector.tensor_copy(out=bias[:], in_=bias_bank[:, 0 : FEATURE_TILES + HALVES])
 
-        def sort_words(b, g):
+        def transpose_in(b, g):
             if g == 0:
                 words = activations[b][0][:].bitcast(F32)
             else:
                 words = activations[b][1][:].bitcast(F32)[:, :, WORDS * (g - 1) : WORDS * g]
-            by_parity = sorted_pool.tile([P, SUBS, 2, P], F32, tag="sorted")
-            nc.scalar.copy(out=by_parity[:], in_=words.rearrange("n s (p u) -> n s u p", u=2))
-            sorted_words[g] = by_parity
-
-        def transpose_in(b, g):
-            words = sorted_words[g]
             grouped_tile = grouped_pool.tile([P, 4 * BLOCK], BF16, tag="grouped", align_bytes=64)
             by_node = grouped_tile[:].bitcast(F32).rearrange("p (s n u) -> p s n u", s=SUBS, u=2)
             for pair in range(SUBS // PAIR):
                 bank = psum.tile([P, PAIR, 2, P], F32, tag="bank")
                 for i in range(PAIR):
                     for u in range(2):
-                        nc.tensor.transpose(bank[:, i, u, :], words[:, PAIR * pair + i, u, :], ident[:])
+                        nc.tensor.transpose(bank[:, i, u, :], words[:, PAIR * pair + i, u:WORDS:2], ident[:])
                 nc.scalar.copy(
                     out=by_node[:, PAIR * pair : PAIR * (pair + 1)], in_=bank[:].rearrange("p i u n -> p i n u")
                 )
@@ -157,7 +149,7 @@ def tile_treelstmcell_pa_t_kernel(
             quantised[(b, g)] = (codes, scales)
 
         def input_term(b):
-            mask = mask_all[:, BLOCK * b : BLOCK * (b + 1)].rearrange("q (p s) -> q s p", s=SUBS)
+            mask = activations[b][2][:].rearrange("q (p s) -> q s p", s=SUBS)
             codes, scales = quantised[(b, 0)]
             for half in range(HALVES):
                 xw = psum.tile([P, BLOCK], F32, tag="bank")
@@ -225,17 +217,11 @@ def tile_treelstmcell_pa_t_kernel(
         def is_block(b):
             return 0 <= b < N_BLOCKS
 
-        for n in range(-UNITS - 2, UNITS * N_BLOCKS + 2):
+        for n in range(-UNITS - 1, UNITS * N_BLOCKS + 2):
             b, q = divmod(n, UNITS)
-            if q == 2 and is_block(b + 2):
-                sort_words(b + 2, 0)
-            if q == 3 and is_block(b + 2):
-                sort_words(b + 2, 1)
-            if q == 0 and is_block(b + 1):
-                sort_words(b + 1, 2)
             if q == 3:
                 if is_block(b + 3):
-                    load_activations(b + 3)
+                    load_activations(b + 3, nc.sync)
                 if is_block(b + 2):
                     load_cell_states(b + 2)
 

@@ -73,6 +73,7 @@ def tile_treelstmcell_pa_t_kernel(
         input_terms = {}
         gates = {}
         results = {}
+        waiting_sums = []
 
         def load_activations(b, queue):
             x_sb = loads.tile([P, SUBS, X_DIM], BF16, tag="x")
@@ -195,7 +196,7 @@ def tile_treelstmcell_pa_t_kernel(
             nc.scalar.activation(out=gate[:], in_=z[:], func=SIGMOID, bias=bias[:, ft : ft + 1], scale=1.0)
             gates[(b, child, half)] = gate
 
-        def gated_sum(b, half, pair):
+        def gated_sum(b, half, pair, adder):
             products = sum_pool.tile([P, PAIR, CHILDREN, P], F32, tag="products")
             for i in range(PAIR):
                 s = PAIR * pair + i
@@ -205,9 +206,16 @@ def tile_treelstmcell_pa_t_kernel(
                 nc.vector.tensor_tensor(
                     out=products[:, i], in0=bank[:], in1=cell_states[b][:, s, :, P * half : P * (half + 1)], op=MULT
                 )
+            waiting_sums.append((b, half, pair, products))
+            if adder is not None:
+                for job in waiting_sums:
+                    child_sum(adder, *job)
+                waiting_sums.clear()
+
+        def child_sum(adder, b, half, pair, products):
             two = sum_pool.tile([P, PAIR, 2, P], F32, tag="two")
-            nc.gpsimd.tensor_tensor(out=two[:], in0=products[:, :, 0:2, :], in1=products[:, :, 2:4, :], op=ADD)
-            nc.gpsimd.tensor_tensor(
+            adder.tensor_tensor(out=two[:], in0=products[:, :, 0:2, :], in1=products[:, :, 2:4, :], op=ADD)
+            adder.tensor_tensor(
                 out=results[b][:, PAIR * pair : PAIR * (pair + 1), P * half : P * (half + 1)],
                 in0=two[:, :, 0, :],
                 in1=two[:, :, 1, :],
@@ -236,9 +244,17 @@ def tile_treelstmcell_pa_t_kernel(
                 if back_q == 0:
                     out_sb = out_pool.tile([P, SUBS, H_DIM], F32, tag="out")
                     results[back_b] = out_sb
-                gated_sum(back_b, back_q // 2, back_q % 2)
-                if back_q == UNITS - 1:
-                    nc.sync.dma_start(out=out_blocks[back_b], in_=results[back_b][:])
+                last_block_end = back_b == N_BLOCKS - 1 and back_q >= 2
+                if not last_block_end:
+                    gated_sum(back_b, back_q // 2, back_q % 2, nc.gpsimd)
+                    if back_q == UNITS - 1:
+                        nc.sync.dma_start(out=out_blocks[back_b], in_=results[back_b][:])
+                else:
+                    gated_sum(back_b, back_q // 2, back_q % 2, nc.vector if back_q == UNITS - 1 else None)
+                    if back_q == UNITS - 1:
+                        for pair in range(SUBS // PAIR):
+                            rows = slice(PAIR * pair, PAIR * (pair + 1))
+                            nc.sync.dma_start(out=out_blocks[back_b][:, rows, :], in_=results[back_b][:, rows, :])
 
             if is_block(b + 1):
                 if q == 0:

@@ -60,9 +60,10 @@ def tile_treelstmcell_pa_t_kernel(
         grouped_pool = ctx.enter_context(tc.tile_pool(name="grouped", bufs=GROUPS))
         quant_pool = ctx.enter_context(tc.tile_pool(name="quant", bufs=2 * GROUPS))
         fi_pool = ctx.enter_context(tc.tile_pool(name="fi", bufs=2 * HALVES))
-        z_pool = ctx.enter_context(tc.tile_pool(name="z", bufs=3))
+        z_pool = ctx.enter_context(tc.tile_pool(name="z", bufs=12))
         gate_pool = ctx.enter_context(tc.tile_pool(name="gate", bufs=12))
         sum_pool = ctx.enter_context(tc.tile_pool(name="sum", bufs=3))
+        product_pool = ctx.enter_context(tc.tile_pool(name="product", bufs=2))
         out_pool = ctx.enter_context(tc.tile_pool(name="out", bufs=2))
         psum = ctx.enter_context(tc.psum_pool(name="psum", bufs=8))
 
@@ -74,6 +75,7 @@ def tile_treelstmcell_pa_t_kernel(
         gates = {}
         results = {}
         waiting_sums = []
+        products_of = {}
 
         def load_activations(b, queue):
             x_sb = loads.tile([P, SUBS, X_DIM], BF16, tag="x")
@@ -197,7 +199,10 @@ def tile_treelstmcell_pa_t_kernel(
             gates[(b, child, half)] = gate
 
         def gated_sum(b, half, pair, adder):
-            products = sum_pool.tile([P, PAIR, CHILDREN, P], F32, tag="products")
+            if half == 0 and pair == 0:
+                block_products = product_pool.tile([P, UNITS, PAIR, CHILDREN, P], F32, tag="products")
+                products_of[b] = block_products
+            products = products_of[b][:, HALVES * half + pair]
             for i in range(PAIR):
                 s = PAIR * pair + i
                 bank = psum.tile([P, CHILDREN, P], F32, tag="bank")

@@ -80,8 +80,11 @@ def tile_treelstmcell_pa_t_kernel(
         def load_activations(b, queue):
             x_sb = loads.tile([P, SUBS, X_DIM], BF16, tag="x")
             queue.dma_start(out=x_sb[:], in_=x_blocks[b])
-            h_sb = loads.tile([P, SUBS, HF_DIM], BF16, tag="h")
-            queue.dma_start(out=h_sb[:], in_=h_blocks[b])
+            h_sb = []
+            for g in range(HF_DIM // K_PASS):
+                h_half = loads.tile([P, SUBS, K_PASS], BF16, tag="h%d" % g)
+                queue.dma_start(out=h_half[:], in_=h_blocks[b][:, :, K_PASS * g : K_PASS * (g + 1)])
+                h_sb.append(h_half)
             mask_sb = loads.tile([P, BLOCK], BF16, tag="mask")
             queue.dma_start(out=mask_sb[:], in_=x_mask[BLOCK * b : BLOCK * (b + 1)].partition_broadcast(P))
             activations[b] = (x_sb, h_sb, mask_sb)
@@ -107,6 +110,10 @@ def tile_treelstmcell_pa_t_kernel(
         )
 
         load_activations(0, nc.scalar)
+        warm = const.tile([P, 1], F32)
+        nc.vector.memset(warm[:], 0.0)
+        warm_out = const.tile([P, 1], F32)
+        nc.scalar.activation(out=warm_out[:], in_=warm[:], func=SIGMOID)
         for quad in range(4):
             rows = slice(4 * quad, 4 * quad + 4)
             parts = slice(32 * quad, 32 * quad + 4)
@@ -132,7 +139,7 @@ def tile_treelstmcell_pa_t_kernel(
             if g == 0:
                 words = activations[b][0][:].bitcast(F32)
             else:
-                words = activations[b][1][:].bitcast(F32)[:, :, WORDS * (g - 1) : WORDS * g]
+                words = activations[b][1][g - 1][:].bitcast(F32)
             grouped_tile = grouped_pool.tile([P, 4 * BLOCK], BF16, tag="grouped", align_bytes=64)
             by_node = grouped_tile[:].bitcast(F32).rearrange("p (s n u) -> p s n u", s=SUBS, u=2)
             for pair in range(SUBS // PAIR):
@@ -151,10 +158,10 @@ def tile_treelstmcell_pa_t_kernel(
             nc.vector.quantize_mx(out=codes[:].bitcast(FP8X4), scales=scales[:], in_=grouped[g][:])
             quantised[(b, g)] = (codes, scales)
 
-        def input_term(b):
+        def input_term(b, halves):
             mask = activations[b][2][:].rearrange("q (p s) -> q s p", s=SUBS)
             codes, scales = quantised[(b, 0)]
-            for half in range(HALVES):
+            for half in halves:
                 xw = psum.tile([P, BLOCK], F32, tag="bank")
                 nc.tensor.matmul_mx(
                     out=xw[:],
@@ -230,7 +237,19 @@ def tile_treelstmcell_pa_t_kernel(
         def is_block(b):
             return 0 <= b < N_BLOCKS
 
-        for n in range(-UNITS - 1, UNITS * N_BLOCKS + 2):
+        load_activations(1, nc.sync)
+        load_cell_states(0)
+        transpose_in(0, 0)
+        quantise(0, 0)
+        transpose_in(0, 1)
+        quantise(0, 1)
+        transpose_in(0, 2)
+        input_term(0, [0])
+        quantise(0, 2)
+        input_term(0, [1])
+        load_activations(2, nc.sync)
+        load_cell_states(1)
+        for n in range(0, UNITS * N_BLOCKS + 2):
             b, q = divmod(n, UNITS)
             if q == 3:
                 if is_block(b + 3):
@@ -242,7 +261,7 @@ def tile_treelstmcell_pa_t_kernel(
                 for child in range(PAIR * (q % 2), PAIR * (q % 2) + PAIR):
                     forget_gate(b, child, q // 2)
             if q == 3 and is_block(b + 1):
-                input_term(b + 1)
+                input_term(b + 1, range(HALVES))
 
             back_b, back_q = divmod(n - 2, UNITS)
             if is_block(back_b):
@@ -262,8 +281,10 @@ def tile_treelstmcell_pa_t_kernel(
                             nc.sync.dma_start(out=out_blocks[back_b][:, rows, :], in_=results[back_b][:, rows, :])
 
             if is_block(b + 1):
-                if q == 0:
+                if q == 0 and n != 0:
                     quantise(b + 1, 0)
+                if n == 1:
+                    quantise(1, 0)
                 if q == 1:
                     quantise(b + 1, 1)
                 if q == 2:
@@ -271,6 +292,8 @@ def tile_treelstmcell_pa_t_kernel(
 
             if q == 3 and is_block(b + 2):
                 transpose_in(b + 2, 0)
+            if n == 0:
+                transpose_in(1, 0)
             if q == 0 and is_block(b + 1):
                 transpose_in(b + 1, 1)
             if q == 1 and is_block(b + 1):

@@ -13,6 +13,7 @@ FP4X4 = mybir.dt.float4_e2m1fn_x4
 ADD = mybir.AluOpType.add
 MULT = mybir.AluOpType.mult
 SIGMOID = mybir.ActivationFunctionType.Sigmoid
+COPY = mybir.ActivationFunctionType.Copy
 
 P = 128
 NODES, X_DIM, CHILDREN, H_DIM = 4096, 512, 4, 256
@@ -75,6 +76,7 @@ def tile_treelstmcell_pa_t_kernel(
         gates = {}
         results = {}
         waiting_sums = []
+        twice_mask = {}
         products_of = {}
 
         def load_activations(b, queue):
@@ -158,8 +160,13 @@ def tile_treelstmcell_pa_t_kernel(
             nc.vector.quantize_mx(out=codes[:].bitcast(FP8X4), scales=scales[:], in_=grouped[g][:])
             quantised[(b, g)] = (codes, scales)
 
+        def double_mask(b):
+            doubled = loads.tile([P, BLOCK], BF16, tag="mask2")
+            nc.scalar.activation(out=doubled[:], in_=activations[b][2][:], func=COPY, scale=2.0)
+            twice_mask[b] = doubled
+
         def input_term(b, halves):
-            mask = activations[b][2][:].rearrange("q (p s) -> q s p", s=SUBS)
+            mask = twice_mask[b][:].rearrange("q (p s) -> q s p", s=SUBS)
             codes, scales = quantised[(b, 0)]
             for half in halves:
                 xw = psum.tile([P, BLOCK], F32, tag="bank")
@@ -198,9 +205,7 @@ def tile_treelstmcell_pa_t_kernel(
                     stop=(g == HF_DIM // K_PASS - 1),
                 )
             z = z_pool.tile([P, BLOCK], F32, tag="z")
-            nc.vector.scalar_tensor_tensor(
-                out=z[:], in0=input_terms[(b, half)][:], scalar=2.0, in1=hw[:], op0=MULT, op1=ADD
-            )
+            nc.vector.tensor_tensor(out=z[:], in0=input_terms[(b, half)][:], in1=hw[:], op=ADD)
             gate = gate_pool.tile([P, BLOCK], F32, tag="gate")
             nc.scalar.activation(out=gate[:], in_=z[:], func=SIGMOID, bias=bias[:, ft : ft + 1], scale=1.0)
             gates[(b, child, half)] = gate
@@ -244,6 +249,7 @@ def tile_treelstmcell_pa_t_kernel(
         transpose_in(0, 1)
         quantise(0, 1)
         transpose_in(0, 2)
+        double_mask(0)
         input_term(0, [0])
         quantise(0, 2)
         input_term(0, [1])
@@ -260,6 +266,8 @@ def tile_treelstmcell_pa_t_kernel(
             if is_block(b):
                 for child in range(PAIR * (q % 2), PAIR * (q % 2) + PAIR):
                     forget_gate(b, child, q // 2)
+            if q == 2 and is_block(b + 1):
+                double_mask(b + 1)
             if q == 3 and is_block(b + 1):
                 input_term(b + 1, range(HALVES))
 

@@ -162,7 +162,10 @@ def tile_treelstmcell_pa_t_kernel(
 
         def double_mask(b):
             doubled = loads.tile([P, BLOCK], BF16, tag="mask2")
-            nc.scalar.activation(out=doubled[:], in_=activations[b][2][:], func=COPY, scale=2.0)
+            if b == 0:
+                nc.vector.tensor_scalar_mul(out=doubled[:], in0=activations[b][2][:], scalar1=2.0)
+            else:
+                nc.scalar.activation(out=doubled[:], in_=activations[b][2][:], func=COPY, scale=2.0)
             twice_mask[b] = doubled
 
         def input_term(b, halves):

@@ -28,6 +28,7 @@ HALVES = H_DIM // P
 FEATURE_TILES = CHILDREN * HALVES
 FP4_TILE_BYTES = 2 * P
 PAIR = 2
+SORTED_GROUPS = (1, 2,)
 UNITS = 4
 
 FLOPS = 2 * NODES * X_DIM * H_DIM + 2 * NODES * HF_DIM * HF_DIM
@@ -64,6 +65,7 @@ def tile_treelstmcell_pa_t_kernel(
         z_pool = ctx.enter_context(tc.tile_pool(name="z", bufs=12))
         gate_pool = ctx.enter_context(tc.tile_pool(name="gate", bufs=12))
         sum_pool = ctx.enter_context(tc.tile_pool(name="sum", bufs=3))
+        sorted_pool = ctx.enter_context(tc.tile_pool(name="sorted", bufs=3))
         product_pool = ctx.enter_context(tc.tile_pool(name="product", bufs=2))
         out_pool = ctx.enter_context(tc.tile_pool(name="out", bufs=2))
         psum = ctx.enter_context(tc.psum_pool(name="psum", bufs=8))
@@ -76,6 +78,7 @@ def tile_treelstmcell_pa_t_kernel(
         gates = {}
         results = {}
         waiting_sums = []
+        sorted_words = {}
         twice_mask = {}
         products_of = {}
 
@@ -142,17 +145,32 @@ def tile_treelstmcell_pa_t_kernel(
                 words = activations[b][0][:].bitcast(F32)
             else:
                 words = activations[b][1][g - 1][:].bitcast(F32)
+            ordered = sorted_words.get((b, g))
             grouped_tile = grouped_pool.tile([P, 4 * BLOCK], BF16, tag="grouped", align_bytes=64)
             by_node = grouped_tile[:].bitcast(F32).rearrange("p (s n u) -> p s n u", s=SUBS, u=2)
             for pair in range(SUBS // PAIR):
                 bank = psum.tile([P, PAIR, 2, P], F32, tag="bank")
                 for i in range(PAIR):
                     for u in range(2):
-                        nc.tensor.transpose(bank[:, i, u, :], words[:, PAIR * pair + i, u:WORDS:2], ident[:])
+                        if ordered is None:
+                            nc.tensor.transpose(bank[:, i, u, :], words[:, PAIR * pair + i, u:WORDS:2], ident[:])
+                        else:
+                            nc.tensor.transpose(bank[:, i, u, :], ordered[:, PAIR * pair + i, u, :], ident[:])
                 nc.scalar.copy(
                     out=by_node[:, PAIR * pair : PAIR * (pair + 1)], in_=bank[:].rearrange("p i u n -> p i n u")
                 )
             grouped[g] = grouped_tile
+
+        def sort_words(b, g):
+            if g not in SORTED_GROUPS:
+                return
+            if g == 0:
+                words = activations[b][0][:].bitcast(F32)
+            else:
+                words = activations[b][1][g - 1][:].bitcast(F32)
+            ordered = sorted_pool.tile([P, SUBS, 2, P], F32, tag="sorted")
+            nc.scalar.copy(out=ordered[:], in_=words.rearrange("p s (w u) -> p s u w", u=2))
+            sorted_words[(b, g)] = ordered
 
         def quantise(b, g):
             codes = quant_pool.tile([P, BLOCK], U32, tag="codes", align_bytes=64)
@@ -301,6 +319,12 @@ def tile_treelstmcell_pa_t_kernel(
                 if q == 2:
                     quantise(b + 1, 2)
 
+            if q == 2 and is_block(b + 2):
+                sort_words(b + 2, 0)
+            if q == 3 and is_block(b + 2):
+                sort_words(b + 2, 1)
+            if q == 0 and is_block(b + 1) and n != 0:
+                sort_words(b + 1, 2)
             if q == 3 and is_block(b + 2):
                 transpose_in(b + 2, 0)
             if n == 0:

from contextlib import ExitStack

import concourse.mybir as mybir
from concourse.masks import make_identity

F32 = mybir.dt.float32
BF16 = mybir.dt.bfloat16
I32 = mybir.dt.int32
U32 = mybir.dt.uint32
U8 = mybir.dt.uint8
FP8X4 = mybir.dt.float8_e4m3fn_x4
FP4X4 = mybir.dt.float4_e2m1fn_x4
ADD = mybir.AluOpType.add
MULT = mybir.AluOpType.mult
SIGMOID = mybir.ActivationFunctionType.Sigmoid
COPY = mybir.ActivationFunctionType.Copy

P = 128
NODES, X_DIM, CHILDREN, H_DIM = 4096, 512, 4, 256
HF_DIM = CHILDREN * H_DIM
K_PASS = 512
WORDS = K_PASS // 2
BLOCK = 512
SUBS = BLOCK // P
N_BLOCKS = NODES // BLOCK
GROUPS = 1 + HF_DIM // K_PASS
HALVES = H_DIM // P
FEATURE_TILES = CHILDREN * HALVES
FP4_TILE_BYTES = 2 * P
PAIR = 2
SORTED_GROUPS = (1, 2,)
UNITS = 4

FLOPS = 2 * NODES * X_DIM * H_DIM + 2 * NODES * HF_DIM * HF_DIM


def tile_treelstmcell_pa_t_kernel(
    tc,
    x,
    x_mask,
    neighbour_h,
    neighbour_c,
    W_f_in_words,
    W_f_in_scales,
    b_f_in,
    W_aggr_f_words,
    W_aggr_f_scales,
    b_aggr_f,
    out,
):
    nc = tc.nc

    x_blocks = x.rearrange("(b p s) k -> b p s k", p=P, s=SUBS)
    h_blocks = neighbour_h.rearrange("(b p s) c f -> b p s (c f)", p=P, s=SUBS)
    c_blocks = neighbour_c.rearrange("(b p s) c f -> b p s c f", p=P, s=SUBS)
    out_blocks = out.rearrange("(b p s) j -> b p s j", p=P, s=SUBS)

    with ExitStack() as ctx:
        ctx.enter_context(tc.manual_schedule())
        const = ctx.enter_context(tc.tile_pool(name="const", bufs=1))
        loads = ctx.enter_context(tc.tile_pool(name="loads", bufs=3))
        grouped_pool = ctx.enter_context(tc.tile_pool(name="grouped", bufs=GROUPS))
        quant_pool = ctx.enter_context(tc.tile_pool(name="quant", bufs=2 * GROUPS))
        fi_pool = ctx.enter_context(tc.tile_pool(name="fi", bufs=2 * HALVES))
        z_pool = ctx.enter_context(tc.tile_pool(name="z", bufs=12))
        gate_pool = ctx.enter_context(tc.tile_pool(name="gate", bufs=12))
        sum_pool = ctx.enter_context(tc.tile_pool(name="sum", bufs=3))
        sorted_pool = ctx.enter_context(tc.tile_pool(name="sorted", bufs=3))
        product_pool = ctx.enter_context(tc.tile_pool(name="product", bufs=2))
        out_pool = ctx.enter_context(tc.tile_pool(name="out", bufs=2))
        psum = ctx.enter_context(tc.psum_pool(name="psum", bufs=8))

        activations = {}
        cell_states = {}
        grouped = {}
        quantised = {}
        input_terms = {}
        gates = {}
        results = {}
        waiting_sums = []
        sorted_words = {}
        twice_mask = {}
        products_of = {}

        def load_activations(b, queue):
            x_sb = loads.tile([P, SUBS, X_DIM], BF16, tag="x")
            queue.dma_start(out=x_sb[:], in_=x_blocks[b])
            h_sb = []
            for g in range(HF_DIM // K_PASS):
                h_half = loads.tile([P, SUBS, K_PASS], BF16, tag="h%d" % g)
                queue.dma_start(out=h_half[:], in_=h_blocks[b][:, :, K_PASS * g : K_PASS * (g + 1)])
                h_sb.append(h_half)
            mask_sb = loads.tile([P, BLOCK], BF16, tag="mask")
            queue.dma_start(out=mask_sb[:], in_=x_mask[BLOCK * b : BLOCK * (b + 1)].partition_broadcast(P))
            activations[b] = (x_sb, h_sb, mask_sb)

        def load_cell_states(b):
            c_sb = loads.tile([P, SUBS, CHILDREN, H_DIM], BF16, tag="c")
            nc.sync.dma_start(out=c_sb[:], in_=c_blocks[b])
            cell_states[b] = c_sb

        ident = const.tile([P, P], F32)
        make_identity(nc, ident[:])

        bias_rows = const.tile([P, P], BF16)
        nc.vector.memset(bias_rows[:], 0.0)
        wf_scales = const.tile([P, H_DIM], U8, align_bytes=64)
        nc.vector.memset(wf_scales[:].bitcast(I32), 0)
        w_scales = const.tile([P, HF_DIM // K_PASS, HF_DIM], U8, align_bytes=64)
        nc.vector.memset(w_scales[:].bitcast(I32), 0)

        nc.scalar.dma_start(out=bias_rows[0:FEATURE_TILES, :], in_=b_aggr_f.rearrange("(r c) -> r c", c=P))
        nc.scalar.dma_start(
            out=bias_rows[FEATURE_TILES : FEATURE_TILES + HALVES, :], in_=b_f_in.rearrange("(r c) -> r c", c=P)
        )

        load_activations(0, nc.scalar)
        warm = const.tile([P, 1], F32)
        nc.vector.memset(warm[:], 0.0)
        warm_out = const.tile([P, 1], F32)
        nc.scalar.activation(out=warm_out[:], in_=warm[:], func=SIGMOID)
        for quad in range(4):
            rows = slice(4 * quad, 4 * quad + 4)
            parts = slice(32 * quad, 32 * quad + 4)
            nc.sync.dma_start(out=wf_scales[parts, :].bitcast(I32), in_=W_f_in_scales[0, rows, :].bitcast(I32))
            nc.sync.dma_start(
                out=w_scales[parts, :, :].bitcast(I32),
                in_=W_aggr_f_scales[:, rows, :].rearrange("g r n -> r g n").bitcast(I32),
            )
        wf_words = const.tile([P, 2 * H_DIM], U8, align_bytes=64)
        nc.sync.dma_start(out=wf_words[:].bitcast(I32), in_=W_f_in_words[0].bitcast(I32))
        w_words = const.tile([P, HF_DIM // K_PASS, 2 * HF_DIM], U8, align_bytes=64)
        for g in range(HF_DIM // K_PASS):
            nc.sync.dma_start(out=w_words[:, g, :].bitcast(I32), in_=W_aggr_f_words[g].bitcast(I32))

        bias_rows_f32 = const.tile([P, P], F32)
        nc.vector.tensor_copy(out=bias_rows_f32[:], in_=bias_rows[:])
        bias_bank = psum.tile([P, P], F32, tag="bank")
        nc.tensor.transpose(bias_bank[:], bias_rows_f32[:], ident[:])
        bias = const.tile([P, FEATURE_TILES + HALVES], F32)
        nc.vector.tensor_copy(out=bias[:], in_=bias_bank[:, 0 : FEATURE_TILES + HALVES])

        def transpose_in(b, g):
            if g == 0:
                words = activations[b][0][:].bitcast(F32)
            else:
                words = activations[b][1][g - 1][:].bitcast(F32)
            ordered = sorted_words.get((b, g))
            grouped_tile = grouped_pool.tile([P, 4 * BLOCK], BF16, tag="grouped", align_bytes=64)
            by_node = grouped_tile[:].bitcast(F32).rearrange("p (s n u) -> p s n u", s=SUBS, u=2)
            for pair in range(SUBS // PAIR):
                bank = psum.tile([P, PAIR, 2, P], F32, tag="bank")
                for i in range(PAIR):
                    for u in range(2):
                        if ordered is None:
                            nc.tensor.transpose(bank[:, i, u, :], words[:, PAIR * pair + i, u:WORDS:2], ident[:])
                        else:
                            nc.tensor.transpose(bank[:, i, u, :], ordered[:, PAIR * pair + i, u, :], ident[:])
                nc.scalar.copy(
                    out=by_node[:, PAIR * pair : PAIR * (pair + 1)], in_=bank[:].rearrange("p i u n -> p i n u")
                )
            grouped[g] = grouped_tile

        def sort_words(b, g):
            if g not in SORTED_GROUPS:
                return
            if g == 0:
                words = activations[b][0][:].bitcast(F32)
            else:
                words = activations[b][1][g - 1][:].bitcast(F32)
            ordered = sorted_pool.tile([P, SUBS, 2, P], F32, tag="sorted")
            nc.scalar.copy(out=ordered[:], in_=words.rearrange("p s (w u) -> p s u w", u=2))
            sorted_words[(b, g)] = ordered

        def quantise(b, g):
            codes = quant_pool.tile([P, BLOCK], U32, tag="codes", align_bytes=64)
            scales = quant_pool.tile([P, BLOCK], U8, tag="scales", align_bytes=64)
            nc.vector.quantize_mx(out=codes[:].bitcast(FP8X4), scales=scales[:], in_=grouped[g][:])
            quantised[(b, g)] = (codes, scales)

        def double_mask(b):
            doubled = loads.tile([P, BLOCK], BF16, tag="mask2")
            if b == 0:
                nc.vector.tensor_scalar_mul(out=doubled[:], in0=activations[b][2][:], scalar1=2.0)
            else:
                nc.scalar.activation(out=doubled[:], in_=activations[b][2][:], func=COPY, scale=2.0)
            twice_mask[b] = doubled

        def input_term(b, halves):
            mask = twice_mask[b][:].rearrange("q (p s) -> q s p", s=SUBS)
            codes, scales = quantised[(b, 0)]
            for half in halves:
                xw = psum.tile([P, BLOCK], F32, tag="bank")
                nc.tensor.matmul_mx(
                    out=xw[:],
                    lhsT=wf_words[:, FP4_TILE_BYTES * half : FP4_TILE_BYTES * (half + 1)].bitcast(FP4X4),
                    lhsT_scale=wf_scales[:, P * half : P * (half + 1)],
                    rhs=codes[:].bitcast(FP8X4),
                    rhs_scale=scales[:],
                    start=True,
                    stop=True,
                )
                fi = fi_pool.tile([P, BLOCK], F32, tag="fi")
                nc.vector.scalar_tensor_tensor(
                    out=fi[:].rearrange("q (s p) -> q s p", s=SUBS),
                    in0=xw[:].rearrange("q (s p) -> q s p", s=SUBS),
                    scalar=bias[:, FEATURE_TILES + half : FEATURE_TILES + half + 1],
                    in1=mask,
                    op0=ADD,
                    op1=MULT,
                )
                input_terms[(b, half)] = fi

        def forget_gate(b, child, half):
            ft = HALVES * child + half
            hw = psum.tile([P, BLOCK], F32, tag="bank")
            for g in range(HF_DIM // K_PASS):
                codes, scales = quantised[(b, 1 + g)]
                nc.tensor.matmul_mx(
                    out=hw[:],
                    lhsT=w_words[:, g, FP4_TILE_BYTES * ft : FP4_TILE_BYTES * (ft + 1)].bitcast(FP4X4),
                    lhsT_scale=w_scales[:, g, P * ft : P * (ft + 1)],
                    rhs=codes[:].bitcast(FP8X4),
                    rhs_scale=scales[:],
                    start=(g == 0),
                    stop=(g == HF_DIM // K_PASS - 1),
                )
            z = z_pool.tile([P, BLOCK], F32, tag="z")
            nc.vector.tensor_tensor(out=z[:], in0=input_terms[(b, half)][:], in1=hw[:], op=ADD)
            gate = gate_pool.tile([P, BLOCK], F32, tag="gate")
            nc.scalar.activation(out=gate[:], in_=z[:], func=SIGMOID, bias=bias[:, ft : ft + 1], scale=1.0)
            gates[(b, child, half)] = gate

        def gated_sum(b, half, pair, adder):
            if half == 0 and pair == 0:
                block_products = product_pool.tile([P, UNITS, PAIR, CHILDREN, P], F32, tag="products")
                products_of[b] = block_products
            products = products_of[b][:, HALVES * half + pair]
            for i in range(PAIR):
                s = PAIR * pair + i
                bank = psum.tile([P, CHILDREN, P], F32, tag="bank")
                for child in range(CHILDREN):
                    nc.tensor.transpose(bank[:, child, :], gates[(b, child, half)][:, P * s : P * (s + 1)], ident[:])
                nc.vector.tensor_tensor(
                    out=products[:, i], in0=bank[:], in1=cell_states[b][:, s, :, P * half : P * (half + 1)], op=MULT
                )
            waiting_sums.append((b, half, pair, products))
            if adder is not None:
                for job in waiting_sums:
                    child_sum(adder, *job)
                waiting_sums.clear()

        def child_sum(adder, b, half, pair, products):
            two = sum_pool.tile([P, PAIR, 2, P], F32, tag="two")
            adder.tensor_tensor(out=two[:], in0=products[:, :, 0:2, :], in1=products[:, :, 2:4, :], op=ADD)
            adder.tensor_tensor(
                out=results[b][:, PAIR * pair : PAIR * (pair + 1), P * half : P * (half + 1)],
                in0=two[:, :, 0, :],
                in1=two[:, :, 1, :],
                op=ADD,
            )

        def is_block(b):
            return 0 <= b < N_BLOCKS

        load_activations(1, nc.sync)
        load_cell_states(0)
        transpose_in(0, 0)
        quantise(0, 0)
        transpose_in(0, 1)
        quantise(0, 1)
        transpose_in(0, 2)
        double_mask(0)
        input_term(0, [0])
        quantise(0, 2)
        input_term(0, [1])
        load_activations(2, nc.sync)
        load_cell_states(1)
        for n in range(0, UNITS * N_BLOCKS + 2):
            b, q = divmod(n, UNITS)
            if q == 3:
                if is_block(b + 3):
                    load_activations(b + 3, nc.sync)
                if is_block(b + 2):
                    load_cell_states(b + 2)

            if is_block(b):
                for child in range(PAIR * (q % 2), PAIR * (q % 2) + PAIR):
                    forget_gate(b, child, q // 2)
            if q == 2 and is_block(b + 1):
                double_mask(b + 1)
            if q == 3 and is_block(b + 1):
                input_term(b + 1, range(HALVES))

            back_b, back_q = divmod(n - 2, UNITS)
            if is_block(back_b):
                if back_q == 0:
                    out_sb = out_pool.tile([P, SUBS, H_DIM], F32, tag="out")
                    results[back_b] = out_sb
                last_block_end = back_b == N_BLOCKS - 1 and back_q >= 2
                if not last_block_end:
                    gated_sum(back_b, back_q // 2, back_q % 2, nc.gpsimd)
                    if back_q == UNITS - 1:
                        nc.sync.dma_start(out=out_blocks[back_b], in_=results[back_b][:])
                else:
                    gated_sum(back_b, back_q // 2, back_q % 2, nc.vector if back_q == UNITS - 1 else None)
                    if back_q == UNITS - 1:
                        for pair in range(SUBS // PAIR):
                            rows = slice(PAIR * pair, PAIR * (pair + 1))
                            nc.sync.dma_start(out=out_blocks[back_b][:, rows, :], in_=results[back_b][:, rows, :])

            if is_block(b + 1):
                if q == 0 and n != 0:
                    quantise(b + 1, 0)
                if n == 1:
                    quantise(1, 0)
                if q == 1:
                    quantise(b + 1, 1)
                if q == 2:
                    quantise(b + 1, 2)

            if q == 2 and is_block(b + 2):
                sort_words(b + 2, 0)
            if q == 3 and is_block(b + 2):
                sort_words(b + 2, 1)
            if q == 0 and is_block(b + 1) and n != 0:
                sort_words(b + 1, 2)
            if q == 3 and is_block(b + 2):
                transpose_in(b + 2, 0)
            if n == 0:
                transpose_in(1, 0)
            if q == 0 and is_block(b + 1):
                transpose_in(b + 1, 1)
            if q == 1 and is_block(b + 1):
                transpose_in(b + 1, 2)
